import numpy as np
import ml_dtypes


def mxq(x, axis, fmt="e4m3"):
    dtype, down = {"e4m3": (ml_dtypes.float8_e4m3fn, 7), "e5m2": (ml_dtypes.float8_e5m2, 14)}[fmt]
    v = np.moveaxis(np.asarray(x, np.float32).astype(ml_dtypes.bfloat16).astype(np.float64), axis, -1)
    blocks = v.reshape(v.shape[:-1] + (-1, 32))
    amax = np.abs(blocks).max(-1, keepdims=True)
    byte = np.maximum(np.where(amax > 0, np.frexp(amax)[1] - 1 + 127, 0) - down, 1)
    scale = np.exp2(byte - 127.0)
    codes = (blocks / scale).astype(np.float32).astype(dtype).astype(np.float64)
    return np.moveaxis((codes * scale).reshape(v.shape), -1, axis)


WIDE = False


def mx_kscale(k):
    if not WIDE:
        return np.ones(k)
    levels = np.array([10, -10, 5, -5, 0])
    a = np.random.permutation(np.resize(levels, k // 512 * 4)).reshape(k // 512, 4)
    idx = np.arange(k)
    return np.exp2(a[idx // 512, idx % 128 // 32])


BF16 = ml_dtypes.bfloat16


def bf(x):
    return np.asarray(x, np.float32).astype(BF16)


def f64(x):
    return np.asarray(x).astype(np.float64)


B, NB, NL, NG, NK = 256, 8192, 256, 500, 3
N2 = 2 * NB
L2 = 2 * NL


def relu(v):
    return np.maximum(v, 0.0)


def setup_inputs():
    s, t = mx_kscale(N2), mx_kscale(L2)
    return {'Volt': bf(np.random.standard_normal((B, N2)) * s),
            'IM': bf(np.random.standard_normal((L2, N2)) / np.sqrt(N2) / s[None, :] * t[:, None]),
            'Ybr': bf(np.random.standard_normal((L2, L2)) / np.sqrt(L2) / t[None, :]),
            'L_limit': bf(np.random.random_sample((NL,)) + 0.5),
            'n_o_mu_i_u': bf(np.random.standard_normal((B, NL)))}


def reference(Volt, IM, Ybr, L_limit, n_o_mu_i_u):
    d = mxq(f64(Volt), 1, 'e4m3') @ mxq(f64(IM), 1, 'e4m3').T
    Ibr = mxq(d, 1, 'e4m3') @ mxq(f64(Ybr), 1, 'e4m3').T
    m = Ibr[:, :NL] ** 2 + Ibr[:, NL:] ** 2
    g = m - f64(L_limit) ** 2
    mu = f64(n_o_mu_i_u)
    return relu(g).sum(axis=1) + np.abs(mu * g).sum(axis=1) + relu(-mu).sum(axis=1)

@@ -1,0 +1,283 @@
+from contextlib import ExitStack
+
+import concourse.mybir as mybir
+from concourse.masks import make_identity
+
+F32 = mybir.dt.float32
+BF16 = mybir.dt.bfloat16
+U32 = mybir.dt.uint32
+U8 = mybir.dt.uint8
+FP8X4 = mybir.dt.float8_e4m3fn_x4
+ALU = mybir.AluOpType
+ACT = mybir.ActivationFunctionType
+
+P = 128
+K_PASS = 512
+WORDS = K_PASS // 2
+
+BATCH = 256
+N2 = 16384
+L2 = 512
+NL = L2 // 2
+
+VOLT_TILES = BATCH // P
+IM_TILES = L2 // P
+CHUNK = 4096
+CHUNKS = N2 // CHUNK
+PASSES = CHUNK // K_PASS
+QUANT_COLS = 2048
+
+FLOPS = 2 * BATCH * L2 * N2 + 2 * BATCH * L2 * L2
+
+
+def tile_kktloss_pa_k_kernel(tc, Volt, IM, Ybr, L_limit, n_o_mu_i_u, out):
+    nc = tc.nc
+    with ExitStack() as ctx:
+        keep = ctx.enter_context(tc.tile_pool(name="keep", bufs=1))
+        volt_in = ctx.enter_context(tc.tile_pool(name="volt_in", bufs=2))
+        im_in = ctx.enter_context(tc.tile_pool(name="im_in", bufs=2 * IM_TILES))
+        regroup = ctx.enter_context(tc.tile_pool(name="regroup", bufs=3))
+        volt_mx = ctx.enter_context(tc.tile_pool(name="volt_mx", bufs=2))
+        im_mx = ctx.enter_context(tc.tile_pool(name="im_mx", bufs=3))
+        tail = ctx.enter_context(tc.tile_pool(name="tail", bufs=2))
+        sums = ctx.enter_context(tc.psum_pool(name="sums", bufs=1))
+        banks = ctx.enter_context(tc.psum_pool(name="banks", bufs=4))
+        ctx.enter_context(tc.manual_schedule())
+
+        ident = keep.tile([P, P], F32)
+        make_identity(nc, ident[:])
+        ones = keep.tile([P, P], BF16)
+        nc.vector.memset(ones[:], 1.0)
+        result_cols = keep.tile([P, P], F32)
+        nc.vector.memset(result_cols[:], 0.0)
+
+        def quantise_blocks(blocks, codes, scales):
+            grouped = regroup.tile([P, len(blocks) * K_PASS], BF16, align_bytes=64)
+            grouped_words = grouped[:].bitcast(F32).rearrange(
+                "p (n r u) -> p n r u", r=P, u=2
+            )
+            for pair in range(len(blocks) // 2):
+                bank = banks.tile([P, 2, 2, P], F32, tag="bank")
+                for i in range(2):
+                    for u in range(2):
+                        nc.tensor.transpose(
+                            bank[:, i, u, :],
+                            blocks[2 * pair + i][:, u * P : (u + 1) * P],
+                            ident[:],
+                        )
+                copy = nc.vector.tensor_copy if pair % 4 == 2 else nc.scalar.copy
+                copy(
+                    out=grouped_words[:, 2 * pair : 2 * pair + 2],
+                    in_=bank[:].rearrange("p i u r -> p i r u"),
+                )
+            for first in range(0, len(blocks) * K_PASS, QUANT_COLS):
+                packed = slice(first // 4, (first + QUANT_COLS) // 4)
+                nc.vector.quantize_mx(
+                    out=codes[:, packed].bitcast(FP8X4),
+                    scales=scales[:, packed],
+                    in_=grouped[:, first : first + QUANT_COLS],
+                )
+
+        ybr_raw = keep.tile([P, IM_TILES * L2], BF16)
+        nc.sync.dma_start(
+            out=ybr_raw[:].rearrange("p (t j) -> p t j", t=IM_TILES),
+            in_=Ybr.rearrange("(t p) j -> p t j", p=P),
+        )
+        limit_row = keep.tile([P, NL], BF16)
+        nc.vector.memset(limit_row[:], 0.0)
+        nc.sync.dma_start(
+            out=limit_row[0:1, :], in_=L_limit.rearrange("(o l) -> o l", o=1)
+        )
+        mu = keep.tile([P, VOLT_TILES * NL], BF16)
+        nc.sync.dma_start(
+            out=mu[:].rearrange("p (t l) -> p t l", t=VOLT_TILES),
+            in_=n_o_mu_i_u.rearrange("(t p) l -> p t l", p=P),
+        )
+
+        volt_rows = Volt.rearrange("(t p) k -> p t k", p=P)
+        im_rows = IM.rearrange("(u p e) k -> u e p k", u=2, e=2)
+
+        def load_chunk(c):
+            cols = slice(c * CHUNK, (c + 1) * CHUNK)
+            volt_raw = volt_in.tile([P, VOLT_TILES * CHUNK], BF16)
+            nc.sync.dma_start(
+                out=volt_raw[:].rearrange("p (t k) -> p t k", t=VOLT_TILES),
+                in_=volt_rows[:, :, cols],
+            )
+            im_raws = []
+            for t in range(IM_TILES):
+                im_raw = im_in.tile([P, CHUNK], BF16)
+                nc.sync.dma_start(out=im_raw[:], in_=im_rows[t // 2, t % 2, :, cols])
+                im_raws.append(im_raw)
+            return volt_raw, im_raws
+
+        loaded = load_chunk(0)
+
+        ybr_codes = keep.tile([P, L2], U32, align_bytes=64)
+        ybr_scales = keep.tile([P, L2], U8, align_bytes=64)
+        ybr_words = ybr_raw[:].bitcast(F32)
+        quantise_blocks(
+            [ybr_words[:, t * WORDS : (t + 1) * WORDS] for t in range(IM_TILES)],
+            ybr_codes,
+            ybr_scales,
+        )
+
+        limit_all = banks.tile([P, NL], F32, tag="bank")
+        nc.tensor.matmul(
+            out=limit_all[:], lhsT=ones[:], rhs=limit_row[:], start=True, stop=True
+        )
+        limit_sq = keep.tile([P, NL], F32)
+        nc.scalar.activation(out=limit_sq[:], in_=limit_all[:], func=ACT.Square)
+
+        neg_mu_sums = []
+        for bt in range(VOLT_TILES):
+            neg_mu = tail.tile([P, NL], F32)
+            neg_mu_sum = keep.tile([P, 1], F32, name="neg_mu_sum%d" % bt)
+            nc.scalar.activation(
+                out=neg_mu[:],
+                in_=mu[:, bt * NL : (bt + 1) * NL],
+                func=ACT.Relu,
+                scale=-1.0,
+                accum_out=neg_mu_sum[:],
+            )
+            neg_mu_sums.append(neg_mu_sum)
+
+        d_sums = [
+            sums.tile([P, BATCH], F32, name="d_sum%d" % t) for t in range(IM_TILES)
+        ]
+        d_grouped = [
+            keep.tile([P, P, IM_TILES], BF16, name="d_grouped%d" % bt, align_bytes=64)
+            for bt in range(VOLT_TILES)
+        ]
+
+        def multiply(c, t, im_codes, im_scales, volt_codes, volt_scales):
+            for g in range(PASSES):
+                rows = slice(g * P, (g + 1) * P)
+                batch = slice(g * BATCH, (g + 1) * BATCH)
+                nc.tensor.matmul_mx(
+                    out=d_sums[t][:],
+                    lhsT=im_codes[:, rows].bitcast(FP8X4),
+                    lhsT_scale=im_scales[:, rows],
+                    rhs=volt_codes[:, batch].bitcast(FP8X4),
+                    rhs_scale=volt_scales[:, batch],
+                    start=(c == 0 and g == 0),
+                    stop=(c == CHUNKS - 1 and g == PASSES - 1),
+                )
+            if c == CHUNKS - 1:
+                for bt in range(VOLT_TILES):
+                    nc.scalar.copy(
+                        out=d_grouped[bt][:, :, t],
+                        in_=d_sums[t][:, bt * P : (bt + 1) * P],
+                    )
+
+        waiting = None
+        for c in range(CHUNKS):
+            volt_raw, im_raws = loaded
+            if c + 1 < CHUNKS:
+                loaded = load_chunk(c + 1)
+
+            volt_codes = volt_mx.tile([P, PASSES * BATCH], U32, align_bytes=64)
+            volt_scales = volt_mx.tile([P, PASSES * BATCH], U8, align_bytes=64)
+            volt_words = volt_raw[:].bitcast(F32).rearrange(
+                "p (t g w) -> p t g w", t=VOLT_TILES, w=WORDS
+            )
+            step = PASSES // VOLT_TILES
+            for first in range(0, PASSES, step):
+                packed = slice(first * BATCH, (first + step) * BATCH)
+                quantise_blocks(
+                    [
+                        volt_words[:, bt, g, :]
+                        for g in range(first, first + step)
+                        for bt in range(VOLT_TILES)
+                    ],
+                    volt_codes[:, packed],
+                    volt_scales[:, packed],
+                )
+
+            for t in range(IM_TILES):
+                im_codes = im_mx.tile([P, PASSES * P], U32, align_bytes=64)
+                im_scales = im_mx.tile([P, PASSES * P], U8, align_bytes=64)
+                im_words = im_raws[t][:].bitcast(F32)
+                quantise_blocks(
+                    [im_words[:, g * WORDS : (g + 1) * WORDS] for g in range(PASSES)],
+                    im_codes,
+                    im_scales,
+                )
+                if waiting is not None:
+                    multiply(*waiting)
+                waiting = (c, t, im_codes, im_scales, volt_codes, volt_scales)
+        multiply(*waiting)
+
+        currents = []
+        for bt in range(VOLT_TILES):
+            d_codes = keep.tile([P, P], U32, name="d_codes%d" % bt, align_bytes=64)
+            d_scales = keep.tile([P, P], U8, name="d_scales%d" % bt, align_bytes=64)
+            nc.vector.quantize_mx(
+                out=d_codes[:].bitcast(FP8X4),
+                scales=d_scales[:],
+                in_=d_grouped[bt][:].rearrange("p b t -> p (b t)"),
+            )
+            ibr = banks.tile([P, L2], F32, tag="bank")
+            nc.tensor.matmul_mx(
+                out=ibr[:],
+                lhsT=d_codes[:].bitcast(FP8X4),
+                lhsT_scale=d_scales[:],
+                rhs=ybr_codes[:].bitcast(FP8X4),
+                rhs_scale=ybr_scales[:],
+                start=True,
+                stop=True,
+            )
+            currents.append(ibr)
+
+        squares = []
+        for bt in range(VOLT_TILES):
+            square = tail.tile([P, L2], F32)
+            nc.scalar.activation(out=square[:], in_=currents[bt][:], func=ACT.Square)
+            squares.append(square)
+
+        for bt in range(VOLT_TILES):
+            magnitude = tail.tile([P, NL], F32)
+            nc.vector.tensor_tensor(
+                out=magnitude[:], in0=squares[bt][:, :NL], in1=squares[bt][:, NL:], op=ALU.add
+            )
+            excess = tail.tile([P, NL], F32)
+            nc.vector.tensor_tensor(
+                out=excess[:], in0=magnitude[:], in1=limit_sq[:], op=ALU.subtract
+            )
+            over = tail.tile([P, NL], F32)
+            over_sum = tail.tile([P, 1], F32)
+            nc.scalar.activation(
+                out=over[:], in_=excess[:], func=ACT.Relu, accum_out=over_sum[:]
+            )
+            slack = tail.tile([P, NL], F32)
+            nc.vector.tensor_tensor(
+                out=slack[:], in0=excess[:], in1=mu[:, bt * NL : (bt + 1) * NL], op=ALU.mult
+            )
+            slack_abs = tail.tile([P, NL], F32)
+            slack_sum = tail.tile([P, 1], F32)
+            nc.vector.scalar_tensor_tensor(
+                out=slack_abs[:],
+                in0=slack[:],
+                scalar=-1.0,
+                in1=slack[:],
+                op0=ALU.mult,
+                op1=ALU.max,
+                accum_out=slack_sum[:],
+            )
+            nc.vector.tensor_scalar(
+                out=result_cols[:, bt : bt + 1],
+                in0=slack_sum[:],
+                scalar1=over_sum[:],
+                scalar2=neg_mu_sums[bt][:],
+                op0=ALU.add,
+                op1=ALU.add,
+            )
+
+        flipped = banks.tile([P, P], F32, tag="bank")
+        nc.tensor.transpose(flipped[:], result_cols[:], ident[:])
+        result_rows = keep.tile([P, P], F32)
+        nc.vector.tensor_copy(out=result_rows[:], in_=flipped[:])
+        nc.sync.dma_start(
+            out=out.rearrange("(t b) -> t b", t=VOLT_TILES),
+            in_=result_rows[0:VOLT_TILES, :],
+        )

@@ -22,12 +22,19 @@ NL = L2 // 2
 
 VOLT_TILES = BATCH // P
 IM_TILES = L2 // P
-CHUNK = 4096
-CHUNKS = N2 // CHUNK
-PASSES = CHUNK // K_PASS
+MAX_CHUNK = 4096
+MIN_CHUNK = 1024
+STAGE_BLOCKS = 8
 QUANT_COLS = 2048
 
 FLOPS = 2 * BATCH * L2 * N2 + 2 * BATCH * L2 * L2
+
+
+def chunk_widths():
+    widths = []
+    while sum(widths) < N2:
+        widths.append(min(MAX_CHUNK, max(MIN_CHUNK, sum(widths))))
+    return widths
 
 
 def tile_kktloss_pa_k_kernel(tc, Volt, IM, Ybr, L_limit, n_o_mu_i_u, out):
@@ -97,16 +104,18 @@ def tile_kktloss_pa_k_kernel(tc, Volt, IM, Ybr, L_limit, n_o_mu_i_u, out):
         volt_rows = Volt.rearrange("(t p) k -> p t k", p=P)
         im_rows = IM.rearrange("(u p e) k -> u e p k", u=2, e=2)
 
+        widths = chunk_widths()
+
         def load_chunk(c):
-            cols = slice(c * CHUNK, (c + 1) * CHUNK)
-            volt_raw = volt_in.tile([P, VOLT_TILES * CHUNK], BF16)
+            cols = slice(sum(widths[:c]), sum(widths[: c + 1]))
+            volt_raw = volt_in.tile([P, VOLT_TILES * widths[c]], BF16)
             nc.sync.dma_start(
                 out=volt_raw[:].rearrange("p (t k) -> p t k", t=VOLT_TILES),
                 in_=volt_rows[:, :, cols],
             )
             im_raws = []
             for t in range(IM_TILES):
-                im_raw = im_in.tile([P, CHUNK], BF16)
+                im_raw = im_in.tile([P, widths[c]], BF16)
                 nc.sync.dma_start(out=im_raw[:], in_=im_rows[t // 2, t % 2, :, cols])
                 im_raws.append(im_raw)
             return volt_raw, im_raws
@@ -150,10 +159,11 @@ def tile_kktloss_pa_k_kernel(tc, Volt, IM, Ybr, L_limit, n_o_mu_i_u, out):
             for bt in range(VOLT_TILES)
         ]
 
-        def multiply(c, t, im_codes, im_scales, volt_codes, volt_scales):
-            for g in range(PASSES):
-                rows = slice(g * P, (g + 1) * P)
+        def multiply(c, blocks, im_codes, im_scales, volt_codes, volt_scales):
+            for n, (t, g) in enumerate(blocks):
+                rows = slice(n * P, (n + 1) * P)
                 batch = slice(g * BATCH, (g + 1) * BATCH)
+                last = c == len(widths) - 1 and g == widths[c] // K_PASS - 1
                 nc.tensor.matmul_mx(
                     out=d_sums[t][:],
                     lhsT=im_codes[:, rows].bitcast(FP8X4),
@@ -161,51 +171,51 @@ def tile_kktloss_pa_k_kernel(tc, Volt, IM, Ybr, L_limit, n_o_mu_i_u, out):
                     rhs=volt_codes[:, batch].bitcast(FP8X4),
                     rhs_scale=volt_scales[:, batch],
                     start=(c == 0 and g == 0),
-                    stop=(c == CHUNKS - 1 and g == PASSES - 1),
+                    stop=last,
                 )
-            if c == CHUNKS - 1:
-                for bt in range(VOLT_TILES):
-                    nc.scalar.copy(
-                        out=d_grouped[bt][:, :, t],
-                        in_=d_sums[t][:, bt * P : (bt + 1) * P],
-                    )
+                if last:
+                    for bt in range(VOLT_TILES):
+                        nc.scalar.copy(
+                            out=d_grouped[bt][:, :, t],
+                            in_=d_sums[t][:, bt * P : (bt + 1) * P],
+                        )
 
         waiting = None
-        for c in range(CHUNKS):
+        for c in range(len(widths)):
+            passes = widths[c] // K_PASS
             volt_raw, im_raws = loaded
-            if c + 1 < CHUNKS:
+            if c + 1 < len(widths):
                 loaded = load_chunk(c + 1)
 
-            volt_codes = volt_mx.tile([P, PASSES * BATCH], U32, align_bytes=64)
-            volt_scales = volt_mx.tile([P, PASSES * BATCH], U8, align_bytes=64)
+            volt_codes = volt_mx.tile([P, passes * BATCH], U32, align_bytes=64)
+            volt_scales = volt_mx.tile([P, passes * BATCH], U8, align_bytes=64)
             volt_words = volt_raw[:].bitcast(F32).rearrange(
                 "p (t g w) -> p t g w", t=VOLT_TILES, w=WORDS
             )
-            step = PASSES // VOLT_TILES
-            for first in range(0, PASSES, step):
-                packed = slice(first * BATCH, (first + step) * BATCH)
+            volt_blocks = [(g, bt) for g in range(passes) for bt in range(VOLT_TILES)]
+            for first in range(0, len(volt_blocks), STAGE_BLOCKS):
+                blocks = volt_blocks[first : first + STAGE_BLOCKS]
+                packed = slice(first * P, (first + len(blocks)) * P)
                 quantise_blocks(
-                    [
-                        volt_words[:, bt, g, :]
-                        for g in range(first, first + step)
-                        for bt in range(VOLT_TILES)
-                    ],
+                    [volt_words[:, bt, g, :] for g, bt in blocks],
                     volt_codes[:, packed],
                     volt_scales[:, packed],
                 )
 
-            for t in range(IM_TILES):
-                im_codes = im_mx.tile([P, PASSES * P], U32, align_bytes=64)
-                im_scales = im_mx.tile([P, PASSES * P], U8, align_bytes=64)
-                im_words = im_raws[t][:].bitcast(F32)
+            im_words = [im_raw[:].bitcast(F32) for im_raw in im_raws]
+            im_blocks = [(t, g) for t in range(IM_TILES) for g in range(passes)]
+            for first in range(0, len(im_blocks), STAGE_BLOCKS):
+                blocks = im_blocks[first : first + STAGE_BLOCKS]
+                im_codes = im_mx.tile([P, STAGE_BLOCKS * P], U32, align_bytes=64)
+                im_scales = im_mx.tile([P, STAGE_BLOCKS * P], U8, align_bytes=64)
                 quantise_blocks(
-                    [im_words[:, g * WORDS : (g + 1) * WORDS] for g in range(PASSES)],
+                    [im_words[t][:, g * WORDS : (g + 1) * WORDS] for t, g in blocks],
                     im_codes,
                     im_scales,
                 )
                 if waiting is not None:
                     multiply(*waiting)
-                waiting = (c, t, im_codes, im_scales, volt_codes, volt_scales)
+                waiting = (c, blocks, im_codes, im_scales, volt_codes, volt_scales)
         multiply(*waiting)
 
         currents = []

@@ -22,19 +22,12 @@ NL = L2 // 2
 
 VOLT_TILES = BATCH // P
 IM_TILES = L2 // P
-MAX_CHUNK = 4096
-MIN_CHUNK = 1024
-STAGE_BLOCKS = 8
+CHUNK = 4096
+CHUNKS = N2 // CHUNK
+PASSES = CHUNK // K_PASS
 QUANT_COLS = 2048
 
 FLOPS = 2 * BATCH * L2 * N2 + 2 * BATCH * L2 * L2
-
-
-def chunk_widths():
-    widths = []
-    while sum(widths) < N2:
-        widths.append(min(MAX_CHUNK, max(MIN_CHUNK, sum(widths))))
-    return widths
 
 
 def tile_kktloss_pa_k_kernel(tc, Volt, IM, Ybr, L_limit, n_o_mu_i_u, out):
@@ -85,51 +78,66 @@ def tile_kktloss_pa_k_kernel(tc, Volt, IM, Ybr, L_limit, n_o_mu_i_u, out):
                     in_=grouped[:, first : first + QUANT_COLS],
                 )
 
-        ybr_raw = keep.tile([P, IM_TILES * L2], BF16)
-        nc.sync.dma_start(
-            out=ybr_raw[:].rearrange("p (t j) -> p t j", t=IM_TILES),
-            in_=Ybr.rearrange("(t p) j -> p t j", p=P),
-        )
         limit_row = keep.tile([P, NL], BF16)
         nc.vector.memset(limit_row[:], 0.0)
-        nc.sync.dma_start(
+        nc.scalar.dma_start(
             out=limit_row[0:1, :], in_=L_limit.rearrange("(o l) -> o l", o=1)
-        )
-        mu = keep.tile([P, VOLT_TILES * NL], BF16)
-        nc.sync.dma_start(
-            out=mu[:].rearrange("p (t l) -> p t l", t=VOLT_TILES),
-            in_=n_o_mu_i_u.rearrange("(t p) l -> p t l", p=P),
         )
 
         volt_rows = Volt.rearrange("(t p) k -> p t k", p=P)
         im_rows = IM.rearrange("(u p e) k -> u e p k", u=2, e=2)
 
-        widths = chunk_widths()
-
         def load_chunk(c):
-            cols = slice(sum(widths[:c]), sum(widths[: c + 1]))
-            volt_raw = volt_in.tile([P, VOLT_TILES * widths[c]], BF16)
+            cols = slice(c * CHUNK, (c + 1) * CHUNK)
+            volt_raw = volt_in.tile([P, VOLT_TILES * CHUNK], BF16)
             nc.sync.dma_start(
                 out=volt_raw[:].rearrange("p (t k) -> p t k", t=VOLT_TILES),
                 in_=volt_rows[:, :, cols],
             )
             im_raws = []
             for t in range(IM_TILES):
-                im_raw = im_in.tile([P, widths[c]], BF16)
+                im_raw = im_in.tile([P, CHUNK], BF16)
                 nc.sync.dma_start(out=im_raw[:], in_=im_rows[t // 2, t % 2, :, cols])
                 im_raws.append(im_raw)
             return volt_raw, im_raws
 
         loaded = load_chunk(0)
 
+        ybr_raw = keep.tile([P, IM_TILES * L2], BF16)
+        mu = keep.tile([P, VOLT_TILES * NL], BF16)
+
+        def load_late_operands():
+            nc.sync.dma_start(
+                out=ybr_raw[:].rearrange("p (t j) -> p t j", t=IM_TILES),
+                in_=Ybr.rearrange("(t p) j -> p t j", p=P),
+            )
+            nc.sync.dma_start(
+                out=mu[:].rearrange("p (t l) -> p t l", t=VOLT_TILES),
+                in_=n_o_mu_i_u.rearrange("(t p) l -> p t l", p=P),
+            )
+
         ybr_codes = keep.tile([P, L2], U32, align_bytes=64)
         ybr_scales = keep.tile([P, L2], U8, align_bytes=64)
-        ybr_words = ybr_raw[:].bitcast(F32)
-        quantise_blocks(
-            [ybr_words[:, t * WORDS : (t + 1) * WORDS] for t in range(IM_TILES)],
-            ybr_codes,
-            ybr_scales,
-        )
+        neg_mu_sums = [
+            keep.tile([P, 1], F32, name="neg_mu_sum%d" % bt) for bt in range(VOLT_TILES)
+        ]
+
+        def prepare_late_operands():
+            ybr_words = ybr_raw[:].bitcast(F32)
+            quantise_blocks(
+                [ybr_words[:, t * WORDS : (t + 1) * WORDS] for t in range(IM_TILES)],
+                ybr_codes,
+                ybr_scales,
+            )
+            for bt in range(VOLT_TILES):
+                neg_mu = tail.tile([P, NL], F32)
+                nc.scalar.activation(
+                    out=neg_mu[:],
+                    in_=mu[:, bt * NL : (bt + 1) * NL],
+                    func=ACT.Relu,
+                    scale=-1.0,
+                    accum_out=neg_mu_sums[bt][:],
+                )
 
         limit_all = banks.tile([P, NL], F32, tag="bank")
         nc.tensor.matmul(
@@ -137,19 +145,6 @@ def tile_kktloss_pa_k_kernel(tc, Volt, IM, Ybr, L_limit, n_o_mu_i_u, out):
         )
         limit_sq = keep.tile([P, NL], F32)
         nc.scalar.activation(out=limit_sq[:], in_=limit_all[:], func=ACT.Square)
-
-        neg_mu_sums = []
-        for bt in range(VOLT_TILES):
-            neg_mu = tail.tile([P, NL], F32)
-            neg_mu_sum = keep.tile([P, 1], F32, name="neg_mu_sum%d" % bt)
-            nc.scalar.activation(
-                out=neg_mu[:],
-                in_=mu[:, bt * NL : (bt + 1) * NL],
-                func=ACT.Relu,
-                scale=-1.0,
-                accum_out=neg_mu_sum[:],
-            )
-            neg_mu_sums.append(neg_mu_sum)
 
         d_sums = [
             sums.tile([P, BATCH], F32, name="d_sum%d" % t) for t in range(IM_TILES)
@@ -159,11 +154,10 @@ def tile_kktloss_pa_k_kernel(tc, Volt, IM, Ybr, L_limit, n_o_mu_i_u, out):
             for bt in range(VOLT_TILES)
         ]
 
-        def multiply(c, blocks, im_codes, im_scales, volt_codes, volt_scales):
-            for n, (t, g) in enumerate(blocks):
-                rows = slice(n * P, (n + 1) * P)
+        def multiply(c, t, im_codes, im_scales, volt_codes, volt_scales):
+            for g in range(PASSES):
+                rows = slice(g * P, (g + 1) * P)
                 batch = slice(g * BATCH, (g + 1) * BATCH)
-                last = c == len(widths) - 1 and g == widths[c] // K_PASS - 1
                 nc.tensor.matmul_mx(
                     out=d_sums[t][:],
                     lhsT=im_codes[:, rows].bitcast(FP8X4),
@@ -171,51 +165,55 @@ def tile_kktloss_pa_k_kernel(tc, Volt, IM, Ybr, L_limit, n_o_mu_i_u, out):
                     rhs=volt_codes[:, batch].bitcast(FP8X4),
                     rhs_scale=volt_scales[:, batch],
                     start=(c == 0 and g == 0),
-                    stop=last,
+                    stop=(c == CHUNKS - 1 and g == PASSES - 1),
                 )
-                if last:
-                    for bt in range(VOLT_TILES):
-                        nc.scalar.copy(
-                            out=d_grouped[bt][:, :, t],
-                            in_=d_sums[t][:, bt * P : (bt + 1) * P],
-                        )
+            if c == CHUNKS - 1:
+                for bt in range(VOLT_TILES):
+                    nc.scalar.copy(
+                        out=d_grouped[bt][:, :, t],
+                        in_=d_sums[t][:, bt * P : (bt + 1) * P],
+                    )
 
         waiting = None
-        for c in range(len(widths)):
-            passes = widths[c] // K_PASS
+        for c in range(CHUNKS):
             volt_raw, im_raws = loaded
-            if c + 1 < len(widths):
+            if c + 1 < CHUNKS:
                 loaded = load_chunk(c + 1)
+            else:
+                load_late_operands()
 
-            volt_codes = volt_mx.tile([P, passes * BATCH], U32, align_bytes=64)
-            volt_scales = volt_mx.tile([P, passes * BATCH], U8, align_bytes=64)
+            volt_codes = volt_mx.tile([P, PASSES * BATCH], U32, align_bytes=64)
+            volt_scales = volt_mx.tile([P, PASSES * BATCH], U8, align_bytes=64)
             volt_words = volt_raw[:].bitcast(F32).rearrange(
                 "p (t g w) -> p t g w", t=VOLT_TILES, w=WORDS
             )
-            volt_blocks = [(g, bt) for g in range(passes) for bt in range(VOLT_TILES)]
-            for first in range(0, len(volt_blocks), STAGE_BLOCKS):
-                blocks = volt_blocks[first : first + STAGE_BLOCKS]
-                packed = slice(first * P, (first + len(blocks)) * P)
+            step = PASSES // VOLT_TILES
+            for first in range(0, PASSES, step):
+                packed = slice(first * BATCH, (first + step) * BATCH)
                 quantise_blocks(
-                    [volt_words[:, bt, g, :] for g, bt in blocks],
+                    [
+                        volt_words[:, bt, g, :]
+                        for g in range(first, first + step)
+                        for bt in range(VOLT_TILES)
+                    ],
                     volt_codes[:, packed],
                     volt_scales[:, packed],
                 )
 
-            im_words = [im_raw[:].bitcast(F32) for im_raw in im_raws]
-            im_blocks = [(t, g) for t in range(IM_TILES) for g in range(passes)]
-            for first in range(0, len(im_blocks), STAGE_BLOCKS):
-                blocks = im_blocks[first : first + STAGE_BLOCKS]
-                im_codes = im_mx.tile([P, STAGE_BLOCKS * P], U32, align_bytes=64)
-                im_scales = im_mx.tile([P, STAGE_BLOCKS * P], U8, align_bytes=64)
+            for t in range(IM_TILES):
+                im_codes = im_mx.tile([P, PASSES * P], U32, align_bytes=64)
+                im_scales = im_mx.tile([P, PASSES * P], U8, align_bytes=64)
+                im_words = im_raws[t][:].bitcast(F32)
                 quantise_blocks(
-                    [im_words[t][:, g * WORDS : (g + 1) * WORDS] for t, g in blocks],
+                    [im_words[:, g * WORDS : (g + 1) * WORDS] for g in range(PASSES)],
                     im_codes,
                     im_scales,
                 )
+                if c == CHUNKS - 1 and t == IM_TILES - 1:
+                    prepare_late_operands()
                 if waiting is not None:
                     multiply(*waiting)
-                waiting = (c, blocks, im_codes, im_scales, volt_codes, volt_scales)
+                waiting = (c, t, im_codes, im_scales, volt_codes, volt_scales)
         multiply(*waiting)
 
         currents = []

from contextlib import ExitStack

import concourse.mybir as mybir
from concourse.masks import make_identity

F32 = mybir.dt.float32
BF16 = mybir.dt.bfloat16
U32 = mybir.dt.uint32
U8 = mybir.dt.uint8
FP8X4 = mybir.dt.float8_e4m3fn_x4
ALU = mybir.AluOpType
ACT = mybir.ActivationFunctionType

P = 128
K_PASS = 512
WORDS = K_PASS // 2

BATCH = 256
N2 = 16384
L2 = 512
NL = L2 // 2

VOLT_TILES = BATCH // P
IM_TILES = L2 // P
CHUNK = 4096
CHUNKS = N2 // CHUNK
PASSES = CHUNK // K_PASS
QUANT_COLS = 2048

FLOPS = 2 * BATCH * L2 * N2 + 2 * BATCH * L2 * L2


def tile_kktloss_pa_k_kernel(tc, Volt, IM, Ybr, L_limit, n_o_mu_i_u, out):
    nc = tc.nc
    with ExitStack() as ctx:
        keep = ctx.enter_context(tc.tile_pool(name="keep", bufs=1))
        volt_in = ctx.enter_context(tc.tile_pool(name="volt_in", bufs=2))
        im_in = ctx.enter_context(tc.tile_pool(name="im_in", bufs=2 * IM_TILES))
        regroup = ctx.enter_context(tc.tile_pool(name="regroup", bufs=3))
        volt_mx = ctx.enter_context(tc.tile_pool(name="volt_mx", bufs=2))
        im_mx = ctx.enter_context(tc.tile_pool(name="im_mx", bufs=3))
        tail = ctx.enter_context(tc.tile_pool(name="tail", bufs=2))
        sums = ctx.enter_context(tc.psum_pool(name="sums", bufs=1))
        banks = ctx.enter_context(tc.psum_pool(name="banks", bufs=4))
        ctx.enter_context(tc.manual_schedule())

        ident = keep.tile([P, P], F32)
        make_identity(nc, ident[:])
        ones = keep.tile([P, P], BF16)
        nc.vector.memset(ones[:], 1.0)
        result_cols = keep.tile([P, P], F32)
        nc.vector.memset(result_cols[:], 0.0)

        def quantise_blocks(blocks, codes, scales):
            grouped = regroup.tile([P, len(blocks) * K_PASS], BF16, align_bytes=64)
            grouped_words = grouped[:].bitcast(F32).rearrange(
                "p (n r u) -> p n r u", r=P, u=2
            )
            for pair in range(len(blocks) // 2):
                bank = banks.tile([P, 2, 2, P], F32, tag="bank")
                for i in range(2):
                    for u in range(2):
                        nc.tensor.transpose(
                            bank[:, i, u, :],
                            blocks[2 * pair + i][:, u * P : (u + 1) * P],
                            ident[:],
                        )
                copy = nc.vector.tensor_copy if pair % 4 == 2 else nc.scalar.copy
                copy(
                    out=grouped_words[:, 2 * pair : 2 * pair + 2],
                    in_=bank[:].rearrange("p i u r -> p i r u"),
                )
            for first in range(0, len(blocks) * K_PASS, QUANT_COLS):
                packed = slice(first // 4, (first + QUANT_COLS) // 4)
                nc.vector.quantize_mx(
                    out=codes[:, packed].bitcast(FP8X4),
                    scales=scales[:, packed],
                    in_=grouped[:, first : first + QUANT_COLS],
                )

        limit_row = keep.tile([P, NL], BF16)
        nc.vector.memset(limit_row[:], 0.0)
        nc.scalar.dma_start(
            out=limit_row[0:1, :], in_=L_limit.rearrange("(o l) -> o l", o=1)
        )

        volt_rows = Volt.rearrange("(t p) k -> p t k", p=P)
        im_rows = IM.rearrange("(u p e) k -> u e p k", u=2, e=2)

        def load_chunk(c):
            cols = slice(c * CHUNK, (c + 1) * CHUNK)
            volt_raw = volt_in.tile([P, VOLT_TILES * CHUNK], BF16)
            nc.sync.dma_start(
                out=volt_raw[:].rearrange("p (t k) -> p t k", t=VOLT_TILES),
                in_=volt_rows[:, :, cols],
            )
            im_raws = []
            for t in range(IM_TILES):
                im_raw = im_in.tile([P, CHUNK], BF16)
                nc.sync.dma_start(out=im_raw[:], in_=im_rows[t // 2, t % 2, :, cols])
                im_raws.append(im_raw)
            return volt_raw, im_raws

        loaded = load_chunk(0)

        ybr_raw = keep.tile([P, IM_TILES * L2], BF16)
        mu = keep.tile([P, VOLT_TILES * NL], BF16)

        def load_late_operands():
            nc.sync.dma_start(
                out=ybr_raw[:].rearrange("p (t j) -> p t j", t=IM_TILES),
                in_=Ybr.rearrange("(t p) j -> p t j", p=P),
            )
            nc.sync.dma_start(
                out=mu[:].rearrange("p (t l) -> p t l", t=VOLT_TILES),
                in_=n_o_mu_i_u.rearrange("(t p) l -> p t l", p=P),
            )

        ybr_codes = keep.tile([P, L2], U32, align_bytes=64)
        ybr_scales = keep.tile([P, L2], U8, align_bytes=64)
        neg_mu_sums = [
            keep.tile([P, 1], F32, name="neg_mu_sum%d" % bt) for bt in range(VOLT_TILES)
        ]

        def prepare_late_operands():
            ybr_words = ybr_raw[:].bitcast(F32)
            quantise_blocks(
                [ybr_words[:, t * WORDS : (t + 1) * WORDS] for t in range(IM_TILES)],
                ybr_codes,
                ybr_scales,
            )
            for bt in range(VOLT_TILES):
                neg_mu = tail.tile([P, NL], F32)
                nc.scalar.activation(
                    out=neg_mu[:],
                    in_=mu[:, bt * NL : (bt + 1) * NL],
                    func=ACT.Relu,
                    scale=-1.0,
                    accum_out=neg_mu_sums[bt][:],
                )

        limit_all = banks.tile([P, NL], F32, tag="bank")
        nc.tensor.matmul(
            out=limit_all[:], lhsT=ones[:], rhs=limit_row[:], start=True, stop=True
        )
        limit_sq = keep.tile([P, NL], F32)
        nc.scalar.activation(out=limit_sq[:], in_=limit_all[:], func=ACT.Square)

        d_sums = [
            sums.tile([P, BATCH], F32, name="d_sum%d" % t) for t in range(IM_TILES)
        ]
        d_grouped = [
            keep.tile([P, P, IM_TILES], BF16, name="d_grouped%d" % bt, align_bytes=64)
            for bt in range(VOLT_TILES)
        ]

        def multiply(c, t, im_codes, im_scales, volt_codes, volt_scales):
            for g in range(PASSES):
                rows = slice(g * P, (g + 1) * P)
                batch = slice(g * BATCH, (g + 1) * BATCH)
                nc.tensor.matmul_mx(
                    out=d_sums[t][:],
                    lhsT=im_codes[:, rows].bitcast(FP8X4),
                    lhsT_scale=im_scales[:, rows],
                    rhs=volt_codes[:, batch].bitcast(FP8X4),
                    rhs_scale=volt_scales[:, batch],
                    start=(c == 0 and g == 0),
                    stop=(c == CHUNKS - 1 and g == PASSES - 1),
                )
            if c == CHUNKS - 1:
                for bt in range(VOLT_TILES):
                    nc.scalar.copy(
                        out=d_grouped[bt][:, :, t],
                        in_=d_sums[t][:, bt * P : (bt + 1) * P],
                    )

        waiting = None
        for c in range(CHUNKS):
            volt_raw, im_raws = loaded
            if c + 1 < CHUNKS:
                loaded = load_chunk(c + 1)
            else:
                load_late_operands()

            volt_codes = volt_mx.tile([P, PASSES * BATCH], U32, align_bytes=64)
            volt_scales = volt_mx.tile([P, PASSES * BATCH], U8, align_bytes=64)
            volt_words = volt_raw[:].bitcast(F32).rearrange(
                "p (t g w) -> p t g w", t=VOLT_TILES, w=WORDS
            )
            step = PASSES // VOLT_TILES
            for first in range(0, PASSES, step):
                packed = slice(first * BATCH, (first + step) * BATCH)
                quantise_blocks(
                    [
                        volt_words[:, bt, g, :]
                        for g in range(first, first + step)
                        for bt in range(VOLT_TILES)
                    ],
                    volt_codes[:, packed],
                    volt_scales[:, packed],
                )

            for t in range(IM_TILES):
                im_codes = im_mx.tile([P, PASSES * P], U32, align_bytes=64)
                im_scales = im_mx.tile([P, PASSES * P], U8, align_bytes=64)
                im_words = im_raws[t][:].bitcast(F32)
                quantise_blocks(
                    [im_words[:, g * WORDS : (g + 1) * WORDS] for g in range(PASSES)],
                    im_codes,
                    im_scales,
                )
                if c == CHUNKS - 1 and t == IM_TILES - 1:
                    prepare_late_operands()
                if waiting is not None:
                    multiply(*waiting)
                waiting = (c, t, im_codes, im_scales, volt_codes, volt_scales)
        multiply(*waiting)

        currents = []
        for bt in range(VOLT_TILES):
            d_codes = keep.tile([P, P], U32, name="d_codes%d" % bt, align_bytes=64)
            d_scales = keep.tile([P, P], U8, name="d_scales%d" % bt, align_bytes=64)
            nc.vector.quantize_mx(
                out=d_codes[:].bitcast(FP8X4),
                scales=d_scales[:],
                in_=d_grouped[bt][:].rearrange("p b t -> p (b t)"),
            )
            ibr = banks.tile([P, L2], F32, tag="bank")
            nc.tensor.matmul_mx(
                out=ibr[:],
                lhsT=d_codes[:].bitcast(FP8X4),
                lhsT_scale=d_scales[:],
                rhs=ybr_codes[:].bitcast(FP8X4),
                rhs_scale=ybr_scales[:],
                start=True,
                stop=True,
            )
            currents.append(ibr)

        squares = []
        for bt in range(VOLT_TILES):
            square = tail.tile([P, L2], F32)
            nc.scalar.activation(out=square[:], in_=currents[bt][:], func=ACT.Square)
            squares.append(square)

        for bt in range(VOLT_TILES):
            magnitude = tail.tile([P, NL], F32)
            nc.vector.tensor_tensor(
                out=magnitude[:], in0=squares[bt][:, :NL], in1=squares[bt][:, NL:], op=ALU.add
            )
            excess = tail.tile([P, NL], F32)
            nc.vector.tensor_tensor(
                out=excess[:], in0=magnitude[:], in1=limit_sq[:], op=ALU.subtract
            )
            over = tail.tile([P, NL], F32)
            over_sum = tail.tile([P, 1], F32)
            nc.scalar.activation(
                out=over[:], in_=excess[:], func=ACT.Relu, accum_out=over_sum[:]
            )
            slack = tail.tile([P, NL], F32)
            nc.vector.tensor_tensor(
                out=slack[:], in0=excess[:], in1=mu[:, bt * NL : (bt + 1) * NL], op=ALU.mult
            )
            slack_abs = tail.tile([P, NL], F32)
            slack_sum = tail.tile([P, 1], F32)
            nc.vector.scalar_tensor_tensor(
                out=slack_abs[:],
                in0=slack[:],
                scalar=-1.0,
                in1=slack[:],
                op0=ALU.mult,
                op1=ALU.max,
                accum_out=slack_sum[:],
            )
            nc.vector.tensor_scalar(
                out=result_cols[:, bt : bt + 1],
                in0=slack_sum[:],
                scalar1=over_sum[:],
                scalar2=neg_mu_sums[bt][:],
                op0=ALU.add,
                op1=ALU.add,
            )

        flipped = banks.tile([P, P], F32, tag="bank")
        nc.tensor.transpose(flipped[:], result_cols[:], ident[:])
        result_rows = keep.tile([P, P], F32)
        nc.vector.tensor_copy(out=result_rows[:], in_=flipped[:])
        nc.sync.dma_start(
            out=out.rearrange("(t b) -> t b", t=VOLT_TILES),
            in_=result_rows[0:VOLT_TILES, :],
        )
